import numpy as np
import ml_dtypes


def mxq(x, axis, fmt="e4m3"):
    dtype, down = {"e4m3": (ml_dtypes.float8_e4m3fn, 7), "e5m2": (ml_dtypes.float8_e5m2, 14)}[fmt]
    v = np.moveaxis(np.asarray(x, np.float32).astype(ml_dtypes.bfloat16).astype(np.float64), axis, -1)
    blocks = v.reshape(v.shape[:-1] + (-1, 32))
    amax = np.abs(blocks).max(-1, keepdims=True)
    byte = np.maximum(np.where(amax > 0, np.frexp(amax)[1] - 1 + 127, 0) - down, 1)
    scale = np.exp2(byte - 127.0)
    codes = (blocks / scale).astype(np.float32).astype(dtype).astype(np.float64)
    return np.moveaxis((codes * scale).reshape(v.shape), -1, axis)


WIDE = False


def mx_kscale(k):
    if not WIDE:
        return np.ones(k)
    levels = np.array([10, -10, 5, -5, 0])
    a = np.random.permutation(np.resize(levels, k // 512 * 4)).reshape(k // 512, 4)
    idx = np.arange(k)
    return np.exp2(a[idx // 512, idx % 128 // 32])


BF16 = ml_dtypes.bfloat16


def bf(x):
    return np.asarray(x, np.float32).astype(BF16)


def f64(x):
    return np.asarray(x).astype(np.float64)


N, DIN, DOUT = 4096, 512, 128
C = 1.0


def sigmoid(v):
    return 1.0 / (1.0 + np.exp(-v))


def lorentz_points(gain, spread):
    t = 1.1 + gain * sigmoid(spread * np.random.standard_normal((N, 1)))
    u = np.random.standard_normal((N, DOUT - 1))
    u = u / np.sqrt(np.sum(u * u, axis=1, keepdims=True))
    return np.concatenate([t, u * np.sqrt(t * t - 1.0)], axis=1)


def setup_inputs():
    s = mx_kscale(N)
    q = lorentz_points(4.0, 0.4)
    q[:, :1] *= -1.0
    k = lorentz_points(4.0, 0.4)
    h = lorentz_points(10.0, 1.0)
    adj = (np.random.random((N, N)) < 0.01) * s[None, :]
    return {"q_neg": bf(q), "k": bf(k), "h": bf(h / s[:, None]), "adj": bf(adj),
            "att_bias": bf(7.0 + 0.2 * np.random.standard_normal(1)),
            "att_scale": bf(2.5 * (1.0 + 0.04 * np.random.standard_normal(1)))}


def reference(q_neg, k, h, adj, att_bias, att_scale):
    cin = f64(q_neg) @ f64(k).T
    att = f64(adj) * sigmoid((2.0 + 2.0 * cin) / f64(att_scale) + f64(att_bias))
    support = mxq(att, 1, "e4m3") @ mxq(f64(h), 0, "e4m3")
    l_inner = -support[:, :1] ** 2 + np.sum(support[:, 1:] ** 2, axis=-1, keepdims=True)
    denom = np.sqrt(np.maximum(np.abs(-l_inner), 1e-6)) / np.sqrt(C)
    return support / denom

@@ -1,0 +1,278 @@
+from contextlib import ExitStack
+
+import concourse.masks as masks
+import concourse.mybir as mybir
+
+F32 = mybir.dt.float32
+BF16 = mybir.dt.bfloat16
+U32 = mybir.dt.uint32
+U8 = mybir.dt.uint8
+FP8X4 = mybir.dt.float8_e4m3fn_x4
+FUNC = mybir.ActivationFunctionType
+ALU = mybir.AluOpType
+
+P = 128
+N = 4096
+D = 128
+PACK = 4
+K_PASS = P * PACK
+N_PASS = N // K_PASS
+N_BLOCKS = N // P
+
+PASSES_PER_UNIT = 2
+UNITS_PER_BLOCK = N_PASS // PASSES_PER_UNIT
+N_UNITS = N_BLOCKS * UNITS_PER_BLOCK
+UNIT_COLS = PASSES_PER_UNIT * P
+UNIT_VALS = UNIT_COLS * PACK
+
+BLOCKS_PER_BATCH = 4
+UNITS_PER_BATCH = BLOCKS_PER_BATCH * UNITS_PER_BLOCK
+N_BATCHES = N_BLOCKS // BLOCKS_PER_BATCH
+
+MX_LAG = 4
+SCALE_LAG = 3
+ADJ_AHEAD = 4
+
+FLOPS = 2 * (2 * N * N * D)
+
+
+def tile_hybonetconv_pb_t_kernel(tc, q_neg, k, h, adj, att_bias, att_scale, out):
+    nc = tc.nc
+
+    q_view = q_neg.rearrange("(p b) d -> p b d", b=N_BLOCKS)
+    adj_view = adj.rearrange("(p b) j -> b p j", b=N_BLOCKS)
+    out_view = out.rearrange("(p b) d -> p b d", b=N_BLOCKS)
+    k_view = k.rearrange("(x p e) d -> p x (e d)", p=P, e=2)
+    h_view = h.rearrange("(x p e) d -> p x (e d)", p=P, e=2)
+
+    with ExitStack() as ctx:
+        const = ctx.enter_context(tc.tile_pool(name="const", bufs=1))
+        adj_pool = ctx.enter_context(tc.tile_pool(name="adj", bufs=ADJ_AHEAD + 1))
+        sig_pool = ctx.enter_context(tc.tile_pool(name="sig", bufs=4))
+        att_pool = ctx.enter_context(tc.tile_pool(name="att", bufs=3))
+        mx_pool = ctx.enter_context(tc.tile_pool(name="mx", bufs=MX_LAG + 2))
+        norm_pool = ctx.enter_context(tc.tile_pool(name="norm", bufs=2))
+
+        q_sb = const.tile([P, N_BLOCKS, D], BF16)
+        nc.sync.dma_start(out=q_sb[:], in_=q_view)
+        k_sb = const.tile([P, N_PASS * PACK, D], BF16)
+        nc.sync.dma_start(out=k_sb[:].rearrange("p (x e) d -> p x (e d)", e=2), in_=k_view)
+
+        adj_tiles = {}
+
+        def load_adj(b):
+            adj_sb = adj_pool.tile([P, N], BF16, name="adj_sb")
+            nc.sync.dma_start(out=adj_sb[:], in_=adj_view[b])
+            adj_tiles[b] = adj_sb
+
+        load_adj(0)
+        h_sb = const.tile([P, N_PASS * PACK, D], BF16)
+        nc.sync.dma_start(out=h_sb[:].rearrange("p (x e) d -> p x (e d)", e=2), in_=h_view)
+        for b in range(1, ADJ_AHEAD):
+            load_adj(b)
+
+        scale_bf = const.tile([P, 1], BF16)
+        nc.scalar.dma_start(out=scale_bf[:], in_=att_scale.partition_broadcast(P))
+        bias_bf = const.tile([P, 1], BF16)
+        nc.scalar.dma_start(out=bias_bf[:], in_=att_bias.partition_broadcast(P))
+
+        ident_bf = const.tile([P, P], BF16)
+        masks.make_identity(nc, ident_bf[:])
+        ident_f32 = const.tile([P, P], F32)
+        masks.make_identity(nc, ident_f32[:])
+        minus_half = const.tile([P, BLOCKS_PER_BATCH], F32)
+        nc.gpsimd.memset(minus_half[:], -0.5)
+
+        sig_scale = const.tile([P, 1], F32)
+        nc.vector.reciprocal(out=sig_scale[:], in_=scale_bf[:])
+        nc.vector.tensor_scalar_mul(out=sig_scale[:], in0=sig_scale[:], scalar1=2.0)
+        sig_bias = const.tile([P, 1], F32)
+        nc.vector.tensor_add(out=sig_bias[:], in0=sig_scale[:], in1=bias_bf[:])
+
+        qT = const.tile([P, N_BLOCKS, P], BF16)
+        kT = const.tile([P, N_PASS * PACK, P], BF16)
+        with tc.psum_pool(name="setup_ps", bufs=4) as setup_ps:
+            for src, dst in ((q_sb, qT), (k_sb, kT)):
+                for first in range(0, N_BLOCKS, 4):
+                    turned = setup_ps.tile([P, 4, P], BF16, name="turned")
+                    for n in range(4):
+                        nc.tensor.transpose(turned[:, n, :], src[:, first + n, :], ident_bf[:])
+                    if (first // 4) % 2 == 0:
+                        nc.vector.tensor_copy(out=dst[:, first : first + 4, :], in_=turned[:])
+                    else:
+                        nc.scalar.copy(out=dst[:, first : first + 4, :], in_=turned[:])
+
+        h_grouped = const.tile([P, N_PASS, D, PACK], BF16, align_bytes=64)
+        nc.vector.tensor_copy(
+            out=h_grouped[:], in_=h_sb[:].rearrange("p (g t) d -> p g d t", t=PACK)
+        )
+        h_words = const.tile([P, N_PASS, D], U32, align_bytes=64)
+        h_scales = const.tile([P, N_PASS, D], U8, align_bytes=64)
+        nc.vector.quantize_mx(
+            out=h_words[:].rearrange("p g d -> p (g d)").bitcast(FP8X4),
+            scales=h_scales[:].rearrange("p g d -> p (g d)"),
+            in_=h_grouped[:].rearrange("p g d t -> p (g d t)"),
+        )
+
+        cin_ps = ctx.enter_context(tc.psum_pool(name="cin_ps", bufs=3))
+        adjT_ps = ctx.enter_context(tc.psum_pool(name="adjT_ps", bufs=3))
+        sup_ps = ctx.enter_context(tc.psum_pool(name="sup_ps", bufs=2))
+
+        adjT_tiles = {}
+        cin_tiles = {}
+        sig_tiles = {}
+        att_tiles = {}
+        word_tiles = {}
+        plane_tiles = {}
+        support_tiles = {}
+        rnorm_tiles = {}
+
+        def transpose_adj(s):
+            b, quarter = divmod(s, UNITS_PER_BLOCK)
+            adj_words = adj_tiles[b][:].bitcast(F32)
+            adjT = adjT_ps.tile([P, 2, PASSES_PER_UNIT, P], F32, name="adjT")
+            for gg in range(PASSES_PER_UNIT):
+                for u in range(2):
+                    x = 2 * (PASSES_PER_UNIT * quarter + gg) + u
+                    nc.tensor.transpose(
+                        adjT[:, u, gg, :], adj_words[:, x * P : (x + 1) * P], ident_f32[:]
+                    )
+            adjT_tiles[s] = adjT
+
+        def scores(s, gg):
+            b, quarter = divmod(s, UNITS_PER_BLOCK)
+            g = PASSES_PER_UNIT * quarter + gg
+            cin = cin_ps.tile([P, PACK, P], F32, name="cin")
+            for t in range(PACK):
+                nc.tensor.matmul(
+                    out=cin[:, t, :],
+                    lhsT=kT[:, PACK * g + t, :],
+                    rhs=qT[:, b, :],
+                    start=True,
+                    stop=True,
+                )
+            cin_tiles[(s, gg)] = cin
+
+        def sigmoid(s):
+            sig = sig_pool.tile([P, UNIT_VALS], F32, name="sig")
+            for gg in range(PASSES_PER_UNIT):
+                nc.scalar.activation(
+                    out=sig[:, gg * K_PASS : (gg + 1) * K_PASS].rearrange(
+                        "p (i t) -> p i t", t=PACK
+                    ),
+                    in_=cin_tiles[(s, gg)][:].rearrange("p t i -> p i t"),
+                    func=FUNC.Sigmoid,
+                    bias=sig_bias[:],
+                    scale=sig_scale[:],
+                )
+            sig_tiles[s] = sig
+
+        def weigh(s):
+            att = att_pool.tile([P, UNIT_VALS], BF16, name="att", align_bytes=64)
+            adjT_bf = adjT_tiles[s][:].rearrange("p u gg i -> p (u gg i)").bitcast(BF16)
+            nc.vector.tensor_tensor(
+                out=att[:].rearrange("p (c u e) -> p c u e", u=2, e=2),
+                in0=sig_tiles[s][:].rearrange("p (c u e) -> p c u e", u=2, e=2),
+                in1=adjT_bf.rearrange("p (u c e) -> p c u e", u=2, e=2),
+                op=ALU.mult,
+            )
+            att_tiles[s] = att
+
+        def quantise(s):
+            words = mx_pool.tile([P, UNIT_COLS], U32, name="words", align_bytes=64)
+            planes = mx_pool.tile([P, UNIT_COLS], U8, name="planes", align_bytes=64)
+            nc.vector.quantize_mx(
+                out=words[:].bitcast(FP8X4), scales=planes[:], in_=att_tiles[s][:]
+            )
+            word_tiles[s] = words
+            plane_tiles[s] = planes
+
+        def aggregate(s):
+            b, quarter = divmod(s, UNITS_PER_BLOCK)
+            batch, slot = divmod(b, BLOCKS_PER_BATCH)
+            if slot == 0 and quarter == 0:
+                support_tiles[batch] = sup_ps.tile([P, BLOCKS_PER_BATCH, D], F32, name="support")
+            words = word_tiles[s]
+            planes = plane_tiles[s]
+            for gg in range(PASSES_PER_UNIT):
+                g = PASSES_PER_UNIT * quarter + gg
+                cols = slice(gg * P, (gg + 1) * P)
+                nc.tensor.matmul_mx(
+                    out=support_tiles[batch][:, slot, :],
+                    lhsT=words[:, cols].bitcast(FP8X4),
+                    lhsT_scale=planes[:, cols],
+                    rhs=h_words[:, g, :].bitcast(FP8X4),
+                    rhs_scale=h_scales[:, g, :],
+                    start=(g == 0),
+                    stop=(g == N_PASS - 1),
+                )
+
+        def norms(batch):
+            support = support_tiles[batch]
+            squares = norm_pool.tile([P, BLOCKS_PER_BATCH, D], F32, name="squares")
+            space2 = norm_pool.tile([P, BLOCKS_PER_BATCH], F32, name="space2")
+            time2 = norm_pool.tile([P, BLOCKS_PER_BATCH], F32, name="time2")
+            for slot in range(BLOCKS_PER_BATCH):
+                nc.scalar.activation(
+                    out=squares[:, slot, 1:D],
+                    in_=support[:, slot, 1:D],
+                    func=FUNC.Square,
+                    accum_out=space2[:, slot : slot + 1],
+                )
+            nc.scalar.activation(out=time2[:], in_=support[:, :, 0], func=FUNC.Square)
+            lorentz = norm_pool.tile([P, BLOCKS_PER_BATCH], F32, name="lorentz")
+            nc.gpsimd.tensor_tensor(out=lorentz[:], in0=space2[:], in1=time2[:], op=ALU.subtract)
+            plus = norm_pool.tile([P, BLOCKS_PER_BATCH], F32, name="plus")
+            nc.gpsimd.tensor_scalar(
+                out=plus[:], in0=lorentz[:], scalar1=0.0, scalar2=None, op0=ALU.max
+            )
+            minus = norm_pool.tile([P, BLOCKS_PER_BATCH], F32, name="minus")
+            nc.gpsimd.tensor_scalar(
+                out=minus[:], in0=lorentz[:], scalar1=-1.0, scalar2=0.0, op0=ALU.mult, op1=ALU.max
+            )
+            size = norm_pool.tile([P, BLOCKS_PER_BATCH], F32, name="size")
+            nc.gpsimd.tensor_tensor(out=size[:], in0=plus[:], in1=minus[:], op=ALU.add)
+            floored = norm_pool.tile([P, BLOCKS_PER_BATCH], F32, name="floored")
+            nc.gpsimd.tensor_scalar(
+                out=floored[:], in0=size[:], scalar1=1e-6, scalar2=None, op0=ALU.max
+            )
+            rnorm = norm_pool.tile([P, BLOCKS_PER_BATCH], F32, name="rnorm")
+            nc.gpsimd.tensor_tensor(out=rnorm[:], in0=floored[:], in1=minus_half[:], op=ALU.pow)
+            rnorm_tiles[batch] = rnorm
+
+        def scale_and_store(batch):
+            support = support_tiles[batch]
+            rnorm = rnorm_tiles[batch]
+            result = norm_pool.tile([P, BLOCKS_PER_BATCH, D], F32, name="result")
+            for slot in range(BLOCKS_PER_BATCH):
+                nc.scalar.activation(
+                    out=result[:, slot, :],
+                    in_=support[:, slot, :],
+                    func=FUNC.Copy,
+                    scale=rnorm[:, slot : slot + 1],
+                )
+            first = batch * BLOCKS_PER_BATCH
+            nc.sync.dma_start(out=out_view[:, first : first + BLOCKS_PER_BATCH, :], in_=result[:])
+
+        with tc.manual_schedule():
+            for step in range(N_UNITS + MX_LAG + SCALE_LAG):
+                if step < N_UNITS:
+                    b, quarter = divmod(step, UNITS_PER_BLOCK)
+                    if quarter == 0 and b + ADJ_AHEAD < N_BLOCKS:
+                        load_adj(b + ADJ_AHEAD)
+                    transpose_adj(step)
+                    scores(step, 0)
+                if 0 <= step - MX_LAG < N_UNITS:
+                    aggregate(step - MX_LAG)
+                if step < N_UNITS:
+                    scores(step, 1)
+                    sigmoid(step)
+                    weigh(step)
+                if 0 <= step - 1 < N_UNITS:
+                    quantise(step - 1)
+                closed, rest = divmod(step - MX_LAG + 1, UNITS_PER_BATCH)
+                if rest == 0 and 1 <= closed <= N_BATCHES:
+                    norms(closed - 1)
+                scaled, rest = divmod(step - MX_LAG - SCALE_LAG + 1, UNITS_PER_BATCH)
+                if rest == 0 and 1 <= scaled <= N_BATCHES:
+                    scale_and_store(scaled - 1)

@@ -24,13 +24,12 @@ UNITS_PER_BLOCK = N_PASS // PASSES_PER_UNIT
 N_UNITS = N_BLOCKS * UNITS_PER_BLOCK
 UNIT_COLS = PASSES_PER_UNIT * P
 UNIT_VALS = UNIT_COLS * PACK
+UNIT_J = PASSES_PER_UNIT * K_PASS
+GROUP = 4
 
-BLOCKS_PER_BATCH = 4
-UNITS_PER_BATCH = BLOCKS_PER_BATCH * UNITS_PER_BLOCK
-N_BATCHES = N_BLOCKS // BLOCKS_PER_BATCH
-
+SCORE_LEAD = 1
 MX_LAG = 4
-SCALE_LAG = 3
+SCALE_LAG = 2
 ADJ_AHEAD = 4
 
 FLOPS = 2 * (2 * N * N * D)
@@ -48,28 +47,35 @@ def tile_hybonetconv_pb_t_kernel(tc, q_neg, k, h, adj, att_bias, att_scale, out)
     with ExitStack() as ctx:
         const = ctx.enter_context(tc.tile_pool(name="const", bufs=1))
         adj_pool = ctx.enter_context(tc.tile_pool(name="adj", bufs=ADJ_AHEAD + 1))
-        sig_pool = ctx.enter_context(tc.tile_pool(name="sig", bufs=4))
+        sig_pool = ctx.enter_context(tc.tile_pool(name="sig", bufs=4 + SCORE_LEAD))
         att_pool = ctx.enter_context(tc.tile_pool(name="att", bufs=3))
         mx_pool = ctx.enter_context(tc.tile_pool(name="mx", bufs=MX_LAG + 2))
-        norm_pool = ctx.enter_context(tc.tile_pool(name="norm", bufs=2))
+        norm_pool = ctx.enter_context(tc.tile_pool(name="norm", bufs=3))
 
+        h_sb = const.tile([P, N_PASS * PACK, D], BF16)
+        nc.sync.dma_start(out=h_sb[:].rearrange("p (x e) d -> p x (e d)", e=2), in_=h_view)
         q_sb = const.tile([P, N_BLOCKS, D], BF16)
-        nc.sync.dma_start(out=q_sb[:], in_=q_view)
+        nc.sync.dma_start(out=q_sb[:, 0:GROUP, :], in_=q_view[:, 0:GROUP, :])
         k_sb = const.tile([P, N_PASS * PACK, D], BF16)
-        nc.sync.dma_start(out=k_sb[:].rearrange("p (x e) d -> p x (e d)", e=2), in_=k_view)
+        k_halves = k_sb[:].rearrange("p (x e) d -> p x (e d)", e=2)
 
         adj_tiles = {}
+        adj_tiles[0] = adj_pool.tile([P, N], BF16, name="adj_sb")
+        for quarter in range(UNITS_PER_BLOCK):
+            halves = slice(2 * PASSES_PER_UNIT * quarter, 2 * PASSES_PER_UNIT * (quarter + 1))
+            nc.sync.dma_start(out=k_halves[:, halves, :], in_=k_view[:, halves, :])
+            cols = slice(UNIT_J * quarter, UNIT_J * (quarter + 1))
+            nc.sync.dma_start(out=adj_tiles[0][:, cols], in_=adj_view[0][:, cols])
 
         def load_adj(b):
             adj_sb = adj_pool.tile([P, N], BF16, name="adj_sb")
             nc.sync.dma_start(out=adj_sb[:], in_=adj_view[b])
             adj_tiles[b] = adj_sb
 
-        load_adj(0)
-        h_sb = const.tile([P, N_PASS * PACK, D], BF16)
-        nc.sync.dma_start(out=h_sb[:].rearrange("p (x e) d -> p x (e d)", e=2), in_=h_view)
-        for b in range(1, ADJ_AHEAD):
-            load_adj(b)
+        load_adj(1)
+        load_adj(2)
+        nc.sync.dma_start(out=q_sb[:, GROUP:N_BLOCKS, :], in_=q_view[:, GROUP:N_BLOCKS, :])
+        load_adj(3)
 
         scale_bf = const.tile([P, 1], BF16)
         nc.scalar.dma_start(out=scale_bf[:], in_=att_scale.partition_broadcast(P))
@@ -80,7 +86,7 @@ def tile_hybonetconv_pb_t_kernel(tc, q_neg, k, h, adj, att_bias, att_scale, out)
         masks.make_identity(nc, ident_bf[:])
         ident_f32 = const.tile([P, P], F32)
         masks.make_identity(nc, ident_f32[:])
-        minus_half = const.tile([P, BLOCKS_PER_BATCH], F32)
+        minus_half = const.tile([P, 1], F32)
         nc.gpsimd.memset(minus_half[:], -0.5)
 
         sig_scale = const.tile([P, 1], F32)
@@ -88,19 +94,6 @@ def tile_hybonetconv_pb_t_kernel(tc, q_neg, k, h, adj, att_bias, att_scale, out)
         nc.vector.tensor_scalar_mul(out=sig_scale[:], in0=sig_scale[:], scalar1=2.0)
         sig_bias = const.tile([P, 1], F32)
         nc.vector.tensor_add(out=sig_bias[:], in0=sig_scale[:], in1=bias_bf[:])
-
-        qT = const.tile([P, N_BLOCKS, P], BF16)
-        kT = const.tile([P, N_PASS * PACK, P], BF16)
-        with tc.psum_pool(name="setup_ps", bufs=4) as setup_ps:
-            for src, dst in ((q_sb, qT), (k_sb, kT)):
-                for first in range(0, N_BLOCKS, 4):
-                    turned = setup_ps.tile([P, 4, P], BF16, name="turned")
-                    for n in range(4):
-                        nc.tensor.transpose(turned[:, n, :], src[:, first + n, :], ident_bf[:])
-                    if (first // 4) % 2 == 0:
-                        nc.vector.tensor_copy(out=dst[:, first : first + 4, :], in_=turned[:])
-                    else:
-                        nc.scalar.copy(out=dst[:, first : first + 4, :], in_=turned[:])
 
         h_grouped = const.tile([P, N_PASS, D, PACK], BF16, align_bytes=64)
         nc.vector.tensor_copy(
@@ -117,6 +110,15 @@ def tile_hybonetconv_pb_t_kernel(tc, q_neg, k, h, adj, att_bias, att_scale, out)
         cin_ps = ctx.enter_context(tc.psum_pool(name="cin_ps", bufs=3))
         adjT_ps = ctx.enter_context(tc.psum_pool(name="adjT_ps", bufs=3))
         sup_ps = ctx.enter_context(tc.psum_pool(name="sup_ps", bufs=2))
+
+        qT = const.tile([P, N_BLOCKS, P], BF16)
+        kT = const.tile([P, N_PASS * PACK, P], BF16)
+
+        def turn(src, dst, first):
+            turned = cin_ps.tile([P, GROUP, P], BF16, name="turned", tag="cin")
+            for n in range(GROUP):
+                nc.tensor.transpose(turned[:, n, :], src[:, first + n, :], ident_bf[:])
+            nc.scalar.copy(out=dst[:, first : first + GROUP, :], in_=turned[:])
 
         adjT_tiles = {}
         cin_tiles = {}
@@ -142,7 +144,7 @@ def tile_hybonetconv_pb_t_kernel(tc, q_neg, k, h, adj, att_bias, att_scale, out)
         def scores(s, gg):
             b, quarter = divmod(s, UNITS_PER_BLOCK)
             g = PASSES_PER_UNIT * quarter + gg
-            cin = cin_ps.tile([P, PACK, P], F32, name="cin")
+            cin = cin_ps.tile([P, PACK, P], F32, name="cin", tag="cin")
             for t in range(PACK):
                 nc.tensor.matmul(
                     out=cin[:, t, :],
@@ -189,16 +191,15 @@ def tile_hybonetconv_pb_t_kernel(tc, q_neg, k, h, adj, att_bias, att_scale, out)
 
         def aggregate(s):
             b, quarter = divmod(s, UNITS_PER_BLOCK)
-            batch, slot = divmod(b, BLOCKS_PER_BATCH)
-            if slot == 0 and quarter == 0:
-                support_tiles[batch] = sup_ps.tile([P, BLOCKS_PER_BATCH, D], F32, name="support")
+            if quarter == 0:
+                support_tiles[b] = sup_ps.tile([P, D], F32, name="support")
             words = word_tiles[s]
             planes = plane_tiles[s]
             for gg in range(PASSES_PER_UNIT):
                 g = PASSES_PER_UNIT * quarter + gg
                 cols = slice(gg * P, (gg + 1) * P)
                 nc.tensor.matmul_mx(
-                    out=support_tiles[batch][:, slot, :],
+                    out=support_tiles[b][:],
                     lhsT=words[:, cols].bitcast(FP8X4),
                     lhsT_scale=planes[:, cols],
                     rhs=h_words[:, g, :].bitcast(FP8X4),
@@ -207,72 +208,64 @@ def tile_hybonetconv_pb_t_kernel(tc, q_neg, k, h, adj, att_bias, att_scale, out)
                     stop=(g == N_PASS - 1),
                 )
 
-        def norms(batch):
-            support = support_tiles[batch]
-            squares = norm_pool.tile([P, BLOCKS_PER_BATCH, D], F32, name="squares")
-            space2 = norm_pool.tile([P, BLOCKS_PER_BATCH], F32, name="space2")
-            time2 = norm_pool.tile([P, BLOCKS_PER_BATCH], F32, name="time2")
-            for slot in range(BLOCKS_PER_BATCH):
-                nc.scalar.activation(
-                    out=squares[:, slot, 1:D],
-                    in_=support[:, slot, 1:D],
-                    func=FUNC.Square,
-                    accum_out=space2[:, slot : slot + 1],
-                )
-            nc.scalar.activation(out=time2[:], in_=support[:, :, 0], func=FUNC.Square)
-            lorentz = norm_pool.tile([P, BLOCKS_PER_BATCH], F32, name="lorentz")
+        def norms(b):
+            support = support_tiles[b]
+            squares = norm_pool.tile([P, D], F32, name="squares")
+            space2 = norm_pool.tile([P, 1], F32, name="space2")
+            time2 = norm_pool.tile([P, 1], F32, name="time2")
+            nc.scalar.activation(
+                out=squares[:, 1:D], in_=support[:, 1:D], func=FUNC.Square, accum_out=space2[:]
+            )
+            nc.scalar.activation(out=time2[:], in_=support[:, 0:1], func=FUNC.Square)
+            lorentz = norm_pool.tile([P, 1], F32, name="lorentz")
             nc.gpsimd.tensor_tensor(out=lorentz[:], in0=space2[:], in1=time2[:], op=ALU.subtract)
-            plus = norm_pool.tile([P, BLOCKS_PER_BATCH], F32, name="plus")
+            size = norm_pool.tile([P, 1], F32, name="size")
             nc.gpsimd.tensor_scalar(
-                out=plus[:], in0=lorentz[:], scalar1=0.0, scalar2=None, op0=ALU.max
+                out=size[:], in0=lorentz[:], scalar1=-1.0, scalar2=lorentz[:], op0=ALU.mult, op1=ALU.max
             )
-            minus = norm_pool.tile([P, BLOCKS_PER_BATCH], F32, name="minus")
-            nc.gpsimd.tensor_scalar(
-                out=minus[:], in0=lorentz[:], scalar1=-1.0, scalar2=0.0, op0=ALU.mult, op1=ALU.max
-            )
-            size = norm_pool.tile([P, BLOCKS_PER_BATCH], F32, name="size")
-            nc.gpsimd.tensor_tensor(out=size[:], in0=plus[:], in1=minus[:], op=ALU.add)
-            floored = norm_pool.tile([P, BLOCKS_PER_BATCH], F32, name="floored")
+            floored = norm_pool.tile([P, 1], F32, name="floored")
             nc.gpsimd.tensor_scalar(
                 out=floored[:], in0=size[:], scalar1=1e-6, scalar2=None, op0=ALU.max
             )
-            rnorm = norm_pool.tile([P, BLOCKS_PER_BATCH], F32, name="rnorm")
+            rnorm = norm_pool.tile([P, 1], F32, name="rnorm")
             nc.gpsimd.tensor_tensor(out=rnorm[:], in0=floored[:], in1=minus_half[:], op=ALU.pow)
-            rnorm_tiles[batch] = rnorm
+            rnorm_tiles[b] = rnorm
 
-        def scale_and_store(batch):
-            support = support_tiles[batch]
-            rnorm = rnorm_tiles[batch]
-            result = norm_pool.tile([P, BLOCKS_PER_BATCH, D], F32, name="result")
-            for slot in range(BLOCKS_PER_BATCH):
-                nc.scalar.activation(
-                    out=result[:, slot, :],
-                    in_=support[:, slot, :],
-                    func=FUNC.Copy,
-                    scale=rnorm[:, slot : slot + 1],
-                )
-            first = batch * BLOCKS_PER_BATCH
-            nc.sync.dma_start(out=out_view[:, first : first + BLOCKS_PER_BATCH, :], in_=result[:])
+        def scale_and_store(b):
+            result = norm_pool.tile([P, D], F32, name="result")
+            nc.scalar.activation(
+                out=result[:], in_=support_tiles[b][:], func=FUNC.Copy, scale=rnorm_tiles[b][:]
+            )
+            nc.sync.dma_start(out=out_view[:, b, :], in_=result[:])
 
         with tc.manual_schedule():
-            for step in range(N_UNITS + MX_LAG + SCALE_LAG):
-                if step < N_UNITS:
+            for step in range(-SCORE_LEAD, N_UNITS + MX_LAG + SCALE_LAG):
+                ahead = step + SCORE_LEAD
+                if 0 <= step < N_UNITS:
                     b, quarter = divmod(step, UNITS_PER_BLOCK)
                     if quarter == 0 and b + ADJ_AHEAD < N_BLOCKS:
                         load_adj(b + ADJ_AHEAD)
                     transpose_adj(step)
-                    scores(step, 0)
+                if ahead < N_UNITS:
+                    b_ahead, quarter_ahead = divmod(ahead, UNITS_PER_BLOCK)
+                    if quarter_ahead == 0 and b_ahead % GROUP == 0:
+                        turn(q_sb, qT, b_ahead)
+                    if b_ahead == 0:
+                        for gg in range(PASSES_PER_UNIT):
+                            turn(k_sb, kT, PACK * (PASSES_PER_UNIT * quarter_ahead + gg))
+                    scores(ahead, 0)
                 if 0 <= step - MX_LAG < N_UNITS:
                     aggregate(step - MX_LAG)
-                if step < N_UNITS:
-                    scores(step, 1)
-                    sigmoid(step)
+                if ahead < N_UNITS:
+                    scores(ahead, 1)
+                    sigmoid(ahead)
+                if 0 <= step < N_UNITS:
                     weigh(step)
                 if 0 <= step - 1 < N_UNITS:
                     quantise(step - 1)
-                closed, rest = divmod(step - MX_LAG + 1, UNITS_PER_BATCH)
-                if rest == 0 and 1 <= closed <= N_BATCHES:
+                closed, rest = divmod(step - MX_LAG + 1, UNITS_PER_BLOCK)
+                if rest == 0 and 1 <= closed <= N_BLOCKS:
                     norms(closed - 1)
-                scaled, rest = divmod(step - MX_LAG - SCALE_LAG + 1, UNITS_PER_BATCH)
-                if rest == 0 and 1 <= scaled <= N_BATCHES:
+                scaled, rest = divmod(step - MX_LAG - SCALE_LAG + 1, UNITS_PER_BLOCK)
+                if rest == 0 and 1 <= scaled <= N_BLOCKS:
                     scale_and_store(scaled - 1)

@@ -26,9 +26,13 @@ UNIT_COLS = PASSES_PER_UNIT * P
 UNIT_VALS = UNIT_COLS * PACK
 UNIT_J = PASSES_PER_UNIT * K_PASS
 GROUP = 4
+PAIR = 2
+N_PAIRS = N_UNITS // PAIR
+PAIRS_PER_BLOCK = UNITS_PER_BLOCK // PAIR
+PASSES_PER_PAIR = PAIR * PASSES_PER_UNIT
 
 SCORE_LEAD = 1
-MX_LAG = 4
+MX_LAG = 6
 SCALE_LAG = 2
 ADJ_AHEAD = 4
 
@@ -49,7 +53,7 @@ def tile_hybonetconv_pb_t_kernel(tc, q_neg, k, h, adj, att_bias, att_scale, out)
         adj_pool = ctx.enter_context(tc.tile_pool(name="adj", bufs=ADJ_AHEAD + 1))
         sig_pool = ctx.enter_context(tc.tile_pool(name="sig", bufs=4 + SCORE_LEAD))
         att_pool = ctx.enter_context(tc.tile_pool(name="att", bufs=3))
-        mx_pool = ctx.enter_context(tc.tile_pool(name="mx", bufs=MX_LAG + 2))
+        mx_pool = ctx.enter_context(tc.tile_pool(name="mx", bufs=MX_LAG // PAIR + 1))
         norm_pool = ctx.enter_context(tc.tile_pool(name="norm", bufs=3))
 
         h_sb = const.tile([P, N_PASS * PACK, D], BF16)
@@ -170,38 +174,40 @@ def tile_hybonetconv_pb_t_kernel(tc, q_neg, k, h, adj, att_bias, att_scale, out)
             sig_tiles[s] = sig
 
         def weigh(s):
-            att = att_pool.tile([P, UNIT_VALS], BF16, name="att", align_bytes=64)
+            pair, half = divmod(s, PAIR)
+            if half == 0:
+                att_tiles[pair] = att_pool.tile(
+                    [P, PAIR, UNIT_VALS], BF16, name="att", align_bytes=64
+                )
             adjT_bf = adjT_tiles[s][:].rearrange("p u gg i -> p (u gg i)").bitcast(BF16)
             nc.vector.tensor_tensor(
-                out=att[:].rearrange("p (c u e) -> p c u e", u=2, e=2),
+                out=att_tiles[pair][:, half, :].rearrange("p (c u e) -> p c u e", u=2, e=2),
                 in0=sig_tiles[s][:].rearrange("p (c u e) -> p c u e", u=2, e=2),
                 in1=adjT_bf.rearrange("p (u c e) -> p c u e", u=2, e=2),
                 op=ALU.mult,
             )
-            att_tiles[s] = att
 
-        def quantise(s):
-            words = mx_pool.tile([P, UNIT_COLS], U32, name="words", align_bytes=64)
-            planes = mx_pool.tile([P, UNIT_COLS], U8, name="planes", align_bytes=64)
+        def quantise(pair):
+            words = mx_pool.tile([P, PASSES_PER_PAIR, P], U32, name="words", align_bytes=64)
+            planes = mx_pool.tile([P, PASSES_PER_PAIR, P], U8, name="planes", align_bytes=64)
             nc.vector.quantize_mx(
-                out=words[:].bitcast(FP8X4), scales=planes[:], in_=att_tiles[s][:]
+                out=words[:].rearrange("p n i -> p (n i)").bitcast(FP8X4),
+                scales=planes[:].rearrange("p n i -> p (n i)"),
+                in_=att_tiles[pair][:].rearrange("p n v -> p (n v)"),
             )
-            word_tiles[s] = words
-            plane_tiles[s] = planes
+            word_tiles[pair] = words
+            plane_tiles[pair] = planes
 
-        def aggregate(s):
-            b, quarter = divmod(s, UNITS_PER_BLOCK)
-            if quarter == 0:
+        def aggregate(pair):
+            b, half_block = divmod(pair, PAIRS_PER_BLOCK)
+            if half_block == 0:
                 support_tiles[b] = sup_ps.tile([P, D], F32, name="support")
-            words = word_tiles[s]
-            planes = plane_tiles[s]
-            for gg in range(PASSES_PER_UNIT):
-                g = PASSES_PER_UNIT * quarter + gg
-                cols = slice(gg * P, (gg + 1) * P)
+            for n in range(PASSES_PER_PAIR):
+                g = PASSES_PER_PAIR * half_block + n
                 nc.tensor.matmul_mx(
                     out=support_tiles[b][:],
-                    lhsT=words[:, cols].bitcast(FP8X4),
-                    lhsT_scale=planes[:, cols],
+                    lhsT=word_tiles[pair][:, n, :].bitcast(FP8X4),
+                    lhsT_scale=plane_tiles[pair][:, n, :],
                     rhs=h_words[:, g, :].bitcast(FP8X4),
                     rhs_scale=h_scales[:, g, :],
                     start=(g == 0),
@@ -211,14 +217,14 @@ def tile_hybonetconv_pb_t_kernel(tc, q_neg, k, h, adj, att_bias, att_scale, out)
         def norms(b):
             support = support_tiles[b]
             squares = norm_pool.tile([P, D], F32, name="squares")
-            space2 = norm_pool.tile([P, 1], F32, name="space2")
-            time2 = norm_pool.tile([P, 1], F32, name="time2")
+            total = norm_pool.tile([P, 1], F32, name="total")
             nc.scalar.activation(
-                out=squares[:, 1:D], in_=support[:, 1:D], func=FUNC.Square, accum_out=space2[:]
+                out=squares[:], in_=support[:], func=FUNC.Square, accum_out=total[:]
             )
-            nc.scalar.activation(out=time2[:], in_=support[:, 0:1], func=FUNC.Square)
             lorentz = norm_pool.tile([P, 1], F32, name="lorentz")
-            nc.gpsimd.tensor_tensor(out=lorentz[:], in0=space2[:], in1=time2[:], op=ALU.subtract)
+            nc.gpsimd.tensor_scalar(
+                out=lorentz[:], in0=squares[:, 0:1], scalar1=-2.0, scalar2=total[:], op0=ALU.mult, op1=ALU.add
+            )
             size = norm_pool.tile([P, 1], F32, name="size")
             nc.gpsimd.tensor_scalar(
                 out=size[:], in0=lorentz[:], scalar1=-1.0, scalar2=lorentz[:], op0=ALU.mult, op1=ALU.max
@@ -239,7 +245,7 @@ def tile_hybonetconv_pb_t_kernel(tc, q_neg, k, h, adj, att_bias, att_scale, out)
             nc.sync.dma_start(out=out_view[:, b, :], in_=result[:])
 
         with tc.manual_schedule():
-            for step in range(-SCORE_LEAD, N_UNITS + MX_LAG + SCALE_LAG):
+            for step in range(-SCORE_LEAD, N_UNITS + MX_LAG + SCALE_LAG - 1):
                 ahead = step + SCORE_LEAD
                 if 0 <= step < N_UNITS:
                     b, quarter = divmod(step, UNITS_PER_BLOCK)
@@ -254,18 +260,20 @@ def tile_hybonetconv_pb_t_kernel(tc, q_neg, k, h, adj, att_bias, att_scale, out)
                         for gg in range(PASSES_PER_UNIT):
                             turn(k_sb, kT, PACK * (PASSES_PER_UNIT * quarter_ahead + gg))
                     scores(ahead, 0)
-                if 0 <= step - MX_LAG < N_UNITS:
-                    aggregate(step - MX_LAG)
+                multiplied, rest = divmod(step - MX_LAG, PAIR)
+                if rest == 0 and 0 <= multiplied < N_PAIRS:
+                    aggregate(multiplied)
                 if ahead < N_UNITS:
                     scores(ahead, 1)
                     sigmoid(ahead)
                 if 0 <= step < N_UNITS:
                     weigh(step)
-                if 0 <= step - 1 < N_UNITS:
-                    quantise(step - 1)
-                closed, rest = divmod(step - MX_LAG + 1, UNITS_PER_BLOCK)
-                if rest == 0 and 1 <= closed <= N_BLOCKS:
-                    norms(closed - 1)
-                scaled, rest = divmod(step - MX_LAG - SCALE_LAG + 1, UNITS_PER_BLOCK)
-                if rest == 0 and 1 <= scaled <= N_BLOCKS:
-                    scale_and_store(scaled - 1)
+                finished, rest = divmod(step - PAIR, PAIR)
+                if rest == 0 and 0 <= finished < N_PAIRS:
+                    quantise(finished)
+                closed, rest = divmod(step - MX_LAG - PAIR, UNITS_PER_BLOCK)
+                if rest == 0 and 0 <= closed < N_BLOCKS:
+                    norms(closed)
+                scaled, rest = divmod(step - MX_LAG - PAIR - SCALE_LAG, UNITS_PER_BLOCK)
+                if rest == 0 and 0 <= scaled < N_BLOCKS:
+                    scale_and_store(scaled)

@@ -26,14 +26,10 @@ UNIT_COLS = PASSES_PER_UNIT * P
 UNIT_VALS = UNIT_COLS * PACK
 UNIT_J = PASSES_PER_UNIT * K_PASS
 GROUP = 4
-PAIR = 2
-N_PAIRS = N_UNITS // PAIR
-PAIRS_PER_BLOCK = UNITS_PER_BLOCK // PAIR
-PASSES_PER_PAIR = PAIR * PASSES_PER_UNIT
 
 SCORE_LEAD = 1
-MX_LAG = 6
-SCALE_LAG = 2
+MX_LAG = 5
+SCALE_LAG = 3
 ADJ_AHEAD = 4
 
 FLOPS = 2 * (2 * N * N * D)
@@ -53,8 +49,8 @@ def tile_hybonetconv_pb_t_kernel(tc, q_neg, k, h, adj, att_bias, att_scale, out)
         adj_pool = ctx.enter_context(tc.tile_pool(name="adj", bufs=ADJ_AHEAD + 1))
         sig_pool = ctx.enter_context(tc.tile_pool(name="sig", bufs=4 + SCORE_LEAD))
         att_pool = ctx.enter_context(tc.tile_pool(name="att", bufs=3))
-        mx_pool = ctx.enter_context(tc.tile_pool(name="mx", bufs=MX_LAG // PAIR + 1))
-        norm_pool = ctx.enter_context(tc.tile_pool(name="norm", bufs=3))
+        mx_pool = ctx.enter_context(tc.tile_pool(name="mx", bufs=MX_LAG + 2))
+        norm_pool = ctx.enter_context(tc.tile_pool(name="norm", bufs=4))
 
         h_sb = const.tile([P, N_PASS * PACK, D], BF16)
         nc.sync.dma_start(out=h_sb[:].rearrange("p (x e) d -> p x (e d)", e=2), in_=h_view)
@@ -174,40 +170,38 @@ def tile_hybonetconv_pb_t_kernel(tc, q_neg, k, h, adj, att_bias, att_scale, out)
             sig_tiles[s] = sig
 
         def weigh(s):
-            pair, half = divmod(s, PAIR)
-            if half == 0:
-                att_tiles[pair] = att_pool.tile(
-                    [P, PAIR, UNIT_VALS], BF16, name="att", align_bytes=64
-                )
+            att = att_pool.tile([P, UNIT_VALS], BF16, name="att", align_bytes=64)
             adjT_bf = adjT_tiles[s][:].rearrange("p u gg i -> p (u gg i)").bitcast(BF16)
             nc.vector.tensor_tensor(
-                out=att_tiles[pair][:, half, :].rearrange("p (c u e) -> p c u e", u=2, e=2),
+                out=att[:].rearrange("p (c u e) -> p c u e", u=2, e=2),
                 in0=sig_tiles[s][:].rearrange("p (c u e) -> p c u e", u=2, e=2),
                 in1=adjT_bf.rearrange("p (u c e) -> p c u e", u=2, e=2),
                 op=ALU.mult,
             )
+            att_tiles[s] = att
 
-        def quantise(pair):
-            words = mx_pool.tile([P, PASSES_PER_PAIR, P], U32, name="words", align_bytes=64)
-            planes = mx_pool.tile([P, PASSES_PER_PAIR, P], U8, name="planes", align_bytes=64)
+        def quantise(s):
+            words = mx_pool.tile([P, UNIT_COLS], U32, name="words", align_bytes=64)
+            planes = mx_pool.tile([P, UNIT_COLS], U8, name="planes", align_bytes=64)
             nc.vector.quantize_mx(
-                out=words[:].rearrange("p n i -> p (n i)").bitcast(FP8X4),
-                scales=planes[:].rearrange("p n i -> p (n i)"),
-                in_=att_tiles[pair][:].rearrange("p n v -> p (n v)"),
+                out=words[:].bitcast(FP8X4), scales=planes[:], in_=att_tiles[s][:]
             )
-            word_tiles[pair] = words
-            plane_tiles[pair] = planes
+            word_tiles[s] = words
+            plane_tiles[s] = planes
 
-        def aggregate(pair):
-            b, half_block = divmod(pair, PAIRS_PER_BLOCK)
-            if half_block == 0:
+        def aggregate(s):
+            b, quarter = divmod(s, UNITS_PER_BLOCK)
+            if quarter == 0:
                 support_tiles[b] = sup_ps.tile([P, D], F32, name="support")
-            for n in range(PASSES_PER_PAIR):
-                g = PASSES_PER_PAIR * half_block + n
+            words = word_tiles[s]
+            planes = plane_tiles[s]
+            for gg in range(PASSES_PER_UNIT):
+                g = PASSES_PER_UNIT * quarter + gg
+                cols = slice(gg * P, (gg + 1) * P)
                 nc.tensor.matmul_mx(
                     out=support_tiles[b][:],
-                    lhsT=word_tiles[pair][:, n, :].bitcast(FP8X4),
-                    lhsT_scale=plane_tiles[pair][:, n, :],
+                    lhsT=words[:, cols].bitcast(FP8X4),
+                    lhsT_scale=planes[:, cols],
                     rhs=h_words[:, g, :].bitcast(FP8X4),
                     rhs_scale=h_scales[:, g, :],
                     start=(g == 0),
@@ -245,7 +239,7 @@ def tile_hybonetconv_pb_t_kernel(tc, q_neg, k, h, adj, att_bias, att_scale, out)
             nc.sync.dma_start(out=out_view[:, b, :], in_=result[:])
 
         with tc.manual_schedule():
-            for step in range(-SCORE_LEAD, N_UNITS + MX_LAG + SCALE_LAG - 1):
+            for step in range(-SCORE_LEAD, N_UNITS + MX_LAG + SCALE_LAG):
                 ahead = step + SCORE_LEAD
                 if 0 <= step < N_UNITS:
                     b, quarter = divmod(step, UNITS_PER_BLOCK)
@@ -260,20 +254,18 @@ def tile_hybonetconv_pb_t_kernel(tc, q_neg, k, h, adj, att_bias, att_scale, out)
                         for gg in range(PASSES_PER_UNIT):
                             turn(k_sb, kT, PACK * (PASSES_PER_UNIT * quarter_ahead + gg))
                     scores(ahead, 0)
-                multiplied, rest = divmod(step - MX_LAG, PAIR)
-                if rest == 0 and 0 <= multiplied < N_PAIRS:
-                    aggregate(multiplied)
+                if 0 <= step - MX_LAG < N_UNITS:
+                    aggregate(step - MX_LAG)
                 if ahead < N_UNITS:
                     scores(ahead, 1)
                     sigmoid(ahead)
                 if 0 <= step < N_UNITS:
                     weigh(step)
-                finished, rest = divmod(step - PAIR, PAIR)
-                if rest == 0 and 0 <= finished < N_PAIRS:
-                    quantise(finished)
-                closed, rest = divmod(step - MX_LAG - PAIR, UNITS_PER_BLOCK)
-                if rest == 0 and 0 <= closed < N_BLOCKS:
-                    norms(closed)
-                scaled, rest = divmod(step - MX_LAG - PAIR - SCALE_LAG, UNITS_PER_BLOCK)
-                if rest == 0 and 0 <= scaled < N_BLOCKS:
-                    scale_and_store(scaled)
+                if 0 <= step - 1 < N_UNITS:
+                    quantise(step - 1)
+                closed, rest = divmod(step - MX_LAG + 1, UNITS_PER_BLOCK)
+                if rest == 0 and 1 <= closed <= N_BLOCKS:
+                    norms(closed - 1)
+                scaled, rest = divmod(step - MX_LAG - SCALE_LAG + 1, UNITS_PER_BLOCK)
+                if rest == 0 and 1 <= scaled <= N_BLOCKS:
+                    scale_and_store(scaled - 1)

from contextlib import ExitStack

import concourse.masks as masks
import concourse.mybir as mybir

F32 = mybir.dt.float32
BF16 = mybir.dt.bfloat16
U32 = mybir.dt.uint32
U8 = mybir.dt.uint8
FP8X4 = mybir.dt.float8_e4m3fn_x4
FUNC = mybir.ActivationFunctionType
ALU = mybir.AluOpType

P = 128
N = 4096
D = 128
PACK = 4
K_PASS = P * PACK
N_PASS = N // K_PASS
N_BLOCKS = N // P

PASSES_PER_UNIT = 2
UNITS_PER_BLOCK = N_PASS // PASSES_PER_UNIT
N_UNITS = N_BLOCKS * UNITS_PER_BLOCK
UNIT_COLS = PASSES_PER_UNIT * P
UNIT_VALS = UNIT_COLS * PACK
UNIT_J = PASSES_PER_UNIT * K_PASS
GROUP = 4

SCORE_LEAD = 1
MX_LAG = 5
SCALE_LAG = 3
ADJ_AHEAD = 4

FLOPS = 2 * (2 * N * N * D)


def tile_hybonetconv_pb_t_kernel(tc, q_neg, k, h, adj, att_bias, att_scale, out):
    nc = tc.nc

    q_view = q_neg.rearrange("(p b) d -> p b d", b=N_BLOCKS)
    adj_view = adj.rearrange("(p b) j -> b p j", b=N_BLOCKS)
    out_view = out.rearrange("(p b) d -> p b d", b=N_BLOCKS)
    k_view = k.rearrange("(x p e) d -> p x (e d)", p=P, e=2)
    h_view = h.rearrange("(x p e) d -> p x (e d)", p=P, e=2)

    with ExitStack() as ctx:
        const = ctx.enter_context(tc.tile_pool(name="const", bufs=1))
        adj_pool = ctx.enter_context(tc.tile_pool(name="adj", bufs=ADJ_AHEAD + 1))
        sig_pool = ctx.enter_context(tc.tile_pool(name="sig", bufs=4 + SCORE_LEAD))
        att_pool = ctx.enter_context(tc.tile_pool(name="att", bufs=3))
        mx_pool = ctx.enter_context(tc.tile_pool(name="mx", bufs=MX_LAG + 2))
        norm_pool = ctx.enter_context(tc.tile_pool(name="norm", bufs=4))

        h_sb = const.tile([P, N_PASS * PACK, D], BF16)
        nc.sync.dma_start(out=h_sb[:].rearrange("p (x e) d -> p x (e d)", e=2), in_=h_view)
        q_sb = const.tile([P, N_BLOCKS, D], BF16)
        nc.sync.dma_start(out=q_sb[:, 0:GROUP, :], in_=q_view[:, 0:GROUP, :])
        k_sb = const.tile([P, N_PASS * PACK, D], BF16)
        k_halves = k_sb[:].rearrange("p (x e) d -> p x (e d)", e=2)

        adj_tiles = {}
        adj_tiles[0] = adj_pool.tile([P, N], BF16, name="adj_sb")
        for quarter in range(UNITS_PER_BLOCK):
            halves = slice(2 * PASSES_PER_UNIT * quarter, 2 * PASSES_PER_UNIT * (quarter + 1))
            nc.sync.dma_start(out=k_halves[:, halves, :], in_=k_view[:, halves, :])
            cols = slice(UNIT_J * quarter, UNIT_J * (quarter + 1))
            nc.sync.dma_start(out=adj_tiles[0][:, cols], in_=adj_view[0][:, cols])

        def load_adj(b):
            adj_sb = adj_pool.tile([P, N], BF16, name="adj_sb")
            nc.sync.dma_start(out=adj_sb[:], in_=adj_view[b])
            adj_tiles[b] = adj_sb

        load_adj(1)
        load_adj(2)
        nc.sync.dma_start(out=q_sb[:, GROUP:N_BLOCKS, :], in_=q_view[:, GROUP:N_BLOCKS, :])
        load_adj(3)

        scale_bf = const.tile([P, 1], BF16)
        nc.scalar.dma_start(out=scale_bf[:], in_=att_scale.partition_broadcast(P))
        bias_bf = const.tile([P, 1], BF16)
        nc.scalar.dma_start(out=bias_bf[:], in_=att_bias.partition_broadcast(P))

        ident_bf = const.tile([P, P], BF16)
        masks.make_identity(nc, ident_bf[:])
        ident_f32 = const.tile([P, P], F32)
        masks.make_identity(nc, ident_f32[:])
        minus_half = const.tile([P, 1], F32)
        nc.gpsimd.memset(minus_half[:], -0.5)

        sig_scale = const.tile([P, 1], F32)
        nc.vector.reciprocal(out=sig_scale[:], in_=scale_bf[:])
        nc.vector.tensor_scalar_mul(out=sig_scale[:], in0=sig_scale[:], scalar1=2.0)
        sig_bias = const.tile([P, 1], F32)
        nc.vector.tensor_add(out=sig_bias[:], in0=sig_scale[:], in1=bias_bf[:])

        h_grouped = const.tile([P, N_PASS, D, PACK], BF16, align_bytes=64)
        nc.vector.tensor_copy(
            out=h_grouped[:], in_=h_sb[:].rearrange("p (g t) d -> p g d t", t=PACK)
        )
        h_words = const.tile([P, N_PASS, D], U32, align_bytes=64)
        h_scales = const.tile([P, N_PASS, D], U8, align_bytes=64)
        nc.vector.quantize_mx(
            out=h_words[:].rearrange("p g d -> p (g d)").bitcast(FP8X4),
            scales=h_scales[:].rearrange("p g d -> p (g d)"),
            in_=h_grouped[:].rearrange("p g d t -> p (g d t)"),
        )

        cin_ps = ctx.enter_context(tc.psum_pool(name="cin_ps", bufs=3))
        adjT_ps = ctx.enter_context(tc.psum_pool(name="adjT_ps", bufs=3))
        sup_ps = ctx.enter_context(tc.psum_pool(name="sup_ps", bufs=2))

        qT = const.tile([P, N_BLOCKS, P], BF16)
        kT = const.tile([P, N_PASS * PACK, P], BF16)

        def turn(src, dst, first):
            turned = cin_ps.tile([P, GROUP, P], BF16, name="turned", tag="cin")
            for n in range(GROUP):
                nc.tensor.transpose(turned[:, n, :], src[:, first + n, :], ident_bf[:])
            nc.scalar.copy(out=dst[:, first : first + GROUP, :], in_=turned[:])

        adjT_tiles = {}
        cin_tiles = {}
        sig_tiles = {}
        att_tiles = {}
        word_tiles = {}
        plane_tiles = {}
        support_tiles = {}
        rnorm_tiles = {}

        def transpose_adj(s):
            b, quarter = divmod(s, UNITS_PER_BLOCK)
            adj_words = adj_tiles[b][:].bitcast(F32)
            adjT = adjT_ps.tile([P, 2, PASSES_PER_UNIT, P], F32, name="adjT")
            for gg in range(PASSES_PER_UNIT):
                for u in range(2):
                    x = 2 * (PASSES_PER_UNIT * quarter + gg) + u
                    nc.tensor.transpose(
                        adjT[:, u, gg, :], adj_words[:, x * P : (x + 1) * P], ident_f32[:]
                    )
            adjT_tiles[s] = adjT

        def scores(s, gg):
            b, quarter = divmod(s, UNITS_PER_BLOCK)
            g = PASSES_PER_UNIT * quarter + gg
            cin = cin_ps.tile([P, PACK, P], F32, name="cin", tag="cin")
            for t in range(PACK):
                nc.tensor.matmul(
                    out=cin[:, t, :],
                    lhsT=kT[:, PACK * g + t, :],
                    rhs=qT[:, b, :],
                    start=True,
                    stop=True,
                )
            cin_tiles[(s, gg)] = cin

        def sigmoid(s):
            sig = sig_pool.tile([P, UNIT_VALS], F32, name="sig")
            for gg in range(PASSES_PER_UNIT):
                nc.scalar.activation(
                    out=sig[:, gg * K_PASS : (gg + 1) * K_PASS].rearrange(
                        "p (i t) -> p i t", t=PACK
                    ),
                    in_=cin_tiles[(s, gg)][:].rearrange("p t i -> p i t"),
                    func=FUNC.Sigmoid,
                    bias=sig_bias[:],
                    scale=sig_scale[:],
                )
            sig_tiles[s] = sig

        def weigh(s):
            att = att_pool.tile([P, UNIT_VALS], BF16, name="att", align_bytes=64)
            adjT_bf = adjT_tiles[s][:].rearrange("p u gg i -> p (u gg i)").bitcast(BF16)
            nc.vector.tensor_tensor(
                out=att[:].rearrange("p (c u e) -> p c u e", u=2, e=2),
                in0=sig_tiles[s][:].rearrange("p (c u e) -> p c u e", u=2, e=2),
                in1=adjT_bf.rearrange("p (u c e) -> p c u e", u=2, e=2),
                op=ALU.mult,
            )
            att_tiles[s] = att

        def quantise(s):
            words = mx_pool.tile([P, UNIT_COLS], U32, name="words", align_bytes=64)
            planes = mx_pool.tile([P, UNIT_COLS], U8, name="planes", align_bytes=64)
            nc.vector.quantize_mx(
                out=words[:].bitcast(FP8X4), scales=planes[:], in_=att_tiles[s][:]
            )
            word_tiles[s] = words
            plane_tiles[s] = planes

        def aggregate(s):
            b, quarter = divmod(s, UNITS_PER_BLOCK)
            if quarter == 0:
                support_tiles[b] = sup_ps.tile([P, D], F32, name="support")
            words = word_tiles[s]
            planes = plane_tiles[s]
            for gg in range(PASSES_PER_UNIT):
                g = PASSES_PER_UNIT * quarter + gg
                cols = slice(gg * P, (gg + 1) * P)
                nc.tensor.matmul_mx(
                    out=support_tiles[b][:],
                    lhsT=words[:, cols].bitcast(FP8X4),
                    lhsT_scale=planes[:, cols],
                    rhs=h_words[:, g, :].bitcast(FP8X4),
                    rhs_scale=h_scales[:, g, :],
                    start=(g == 0),
                    stop=(g == N_PASS - 1),
                )

        def norms(b):
            support = support_tiles[b]
            squares = norm_pool.tile([P, D], F32, name="squares")
            total = norm_pool.tile([P, 1], F32, name="total")
            nc.scalar.activation(
                out=squares[:], in_=support[:], func=FUNC.Square, accum_out=total[:]
            )
            lorentz = norm_pool.tile([P, 1], F32, name="lorentz")
            nc.gpsimd.tensor_scalar(
                out=lorentz[:], in0=squares[:, 0:1], scalar1=-2.0, scalar2=total[:], op0=ALU.mult, op1=ALU.add
            )
            size = norm_pool.tile([P, 1], F32, name="size")
            nc.gpsimd.tensor_scalar(
                out=size[:], in0=lorentz[:], scalar1=-1.0, scalar2=lorentz[:], op0=ALU.mult, op1=ALU.max
            )
            floored = norm_pool.tile([P, 1], F32, name="floored")
            nc.gpsimd.tensor_scalar(
                out=floored[:], in0=size[:], scalar1=1e-6, scalar2=None, op0=ALU.max
            )
            rnorm = norm_pool.tile([P, 1], F32, name="rnorm")
            nc.gpsimd.tensor_tensor(out=rnorm[:], in0=floored[:], in1=minus_half[:], op=ALU.pow)
            rnorm_tiles[b] = rnorm

        def scale_and_store(b):
            result = norm_pool.tile([P, D], F32, name="result")
            nc.scalar.activation(
                out=result[:], in_=support_tiles[b][:], func=FUNC.Copy, scale=rnorm_tiles[b][:]
            )
            nc.sync.dma_start(out=out_view[:, b, :], in_=result[:])

        with tc.manual_schedule():
            for step in range(-SCORE_LEAD, N_UNITS + MX_LAG + SCALE_LAG):
                ahead = step + SCORE_LEAD
                if 0 <= step < N_UNITS:
                    b, quarter = divmod(step, UNITS_PER_BLOCK)
                    if quarter == 0 and b + ADJ_AHEAD < N_BLOCKS:
                        load_adj(b + ADJ_AHEAD)
                    transpose_adj(step)
                if ahead < N_UNITS:
                    b_ahead, quarter_ahead = divmod(ahead, UNITS_PER_BLOCK)
                    if quarter_ahead == 0 and b_ahead % GROUP == 0:
                        turn(q_sb, qT, b_ahead)
                    if b_ahead == 0:
                        for gg in range(PASSES_PER_UNIT):
                            turn(k_sb, kT, PACK * (PASSES_PER_UNIT * quarter_ahead + gg))
                    scores(ahead, 0)
                if 0 <= step - MX_LAG < N_UNITS:
                    aggregate(step - MX_LAG)
                if ahead < N_UNITS:
                    scores(ahead, 1)
                    sigmoid(ahead)
                if 0 <= step < N_UNITS:
                    weigh(step)
                if 0 <= step - 1 < N_UNITS:
                    quantise(step - 1)
                closed, rest = divmod(step - MX_LAG + 1, UNITS_PER_BLOCK)
                if rest == 0 and 1 <= closed <= N_BLOCKS:
                    norms(closed - 1)
                scaled, rest = divmod(step - MX_LAG - SCALE_LAG + 1, UNITS_PER_BLOCK)
                if rest == 0 and 1 <= scaled <= N_BLOCKS:
                    scale_and_store(scaled - 1)
